import numpy as np
import ml_dtypes


def mxq(x, axis, fmt="e4m3"):
    dtype, down = {"e4m3": (ml_dtypes.float8_e4m3fn, 7), "e5m2": (ml_dtypes.float8_e5m2, 14)}[fmt]
    v = np.moveaxis(np.asarray(x, np.float32).astype(ml_dtypes.bfloat16).astype(np.float64), axis, -1)
    blocks = v.reshape(v.shape[:-1] + (-1, 32))
    amax = np.abs(blocks).max(-1, keepdims=True)
    byte = np.maximum(np.where(amax > 0, np.frexp(amax)[1] - 1 + 127, 0) - down, 1)
    scale = np.exp2(byte - 127.0)
    codes = (blocks / scale).astype(np.float32).astype(dtype).astype(np.float64)
    return np.moveaxis((codes * scale).reshape(v.shape), -1, axis)


WIDE = False


def mx_kscale(k):
    if not WIDE:
        return np.ones(k)
    levels = np.array([10, -10, 5, -5, 0])
    if k % 512:
        return np.exp2(np.random.permutation(np.resize(levels, k // 32))).repeat(32)
    a = np.empty((k // 512, 16))
    for p in range(k // 512):
        a[p, :8] = np.random.permutation(np.resize(levels, 8))
        for g in range(8):
            far = levels[np.abs(levels - a[p, g]) >= 10]
            a[p, g + 8] = far[np.random.randint(len(far))]
    return np.exp2(a.ravel()).repeat(32)


BF16 = ml_dtypes.bfloat16


def bf(x):
    return np.asarray(x, np.float32).astype(BF16)


def f64(x):
    return np.asarray(x).astype(np.float64)


B, S, H, D, M = 2, 512, 16, 128, 1024
E = H * D
R = B * S
EPS = 1e-6


def setup_inputs():
    s = mx_kscale(E)
    return {"query_input": bf(np.random.standard_normal((B, S, E))),
            "norm_query_w": bf((1.0 + 0.1 * np.random.standard_normal(E)) * s),
            "W_in": bf(np.random.standard_normal((E, E)) / np.sqrt(E) / s[None, :])}


def reference(query_input, norm_query_w, W_in):
    x = f64(query_input).reshape(R, E)
    normed = x * (1.0 / np.sqrt(np.mean(x * x, 1, keepdims=True) + EPS))
    h = normed * f64(norm_query_w)
    return (mxq(h, 1, "e4m3") @ mxq(f64(W_in), 1, "e4m3").T).reshape(B, S, E)

@@ -1,0 +1,270 @@
+from contextlib import ExitStack
+
+import concourse.mybir as mybir
+from concourse.masks import make_identity
+
+F32 = mybir.dt.float32
+BF16 = mybir.dt.bfloat16
+U32 = mybir.dt.uint32
+U8 = mybir.dt.uint8
+FP8X4 = mybir.dt.float8_e4m3fn_x4
+ACT = mybir.ActivationFunctionType
+ALU = mybir.AluOpType
+
+P = 128
+R = 1024
+E = 2048
+NB = 512
+NH = 256
+EPS = 1e-6
+FLOPS = 2 * R * E * E
+
+LOADS = ("x0", "w0", "x1", "w1", "x2", "x3", "w2", "w3", "x4", "x5", "x6", "x7")
+
+
+def tile_hopfieldmemorylayer_pa_kernel(tc, query_input, norm_query_w, W_in, out):
+    nc = tc.nc
+    x = query_input.flatten_outer_dims()
+    o = out.flatten_outer_dims()
+    with ExitStack() as ctx:
+        const = ctx.enter_context(tc.tile_pool(name="const", bufs=1))
+        xpool = ctx.enter_context(tc.tile_pool(name="xpool", bufs=8))
+        wpool = ctx.enter_context(tc.tile_pool(name="wpool", bufs=16))
+        zpool = ctx.enter_context(tc.tile_pool(name="zpool", bufs=2))
+        small = ctx.enter_context(tc.tile_pool(name="small", bufs=8))
+        ghpool = ctx.enter_context(tc.tile_pool(name="ghpool", bufs=2))
+        gwpool = ctx.enter_context(tc.tile_pool(name="gwpool", bufs=2))
+        respool = ctx.enter_context(tc.tile_pool(name="respool", bufs=8))
+        tps = ctx.enter_context(tc.psum_pool(name="tps", bufs=4))
+        accs = ctx.enter_context(tc.psum_pool(name="accs", bufs=4))
+        ctx.enter_context(tc.manual_schedule())
+
+        ident = const.tile([P, P], F32, name="ident")
+        make_identity(nc, ident[:])
+        eps = const.tile([P, 1], F32, name="eps")
+        nc.vector.memset(eps[:], EPS)
+        warm = const.tile([P, 1], F32, name="warm")
+        nc.scalar.activation(out=warm[:], in_=eps[:], func=ACT.Sqrt)
+        graw = const.tile([P, NB], BF16, name="graw")
+        nc.vector.memset(graw[:], 0.0)
+        nc.sync.dma_start(out=graw[0:4, :], in_=norm_query_w.rearrange("(c w) -> c w", w=NB))
+        junk = const.tile([P, E], BF16, name="junk")
+        g_t = const.tile([P, 16], F32, name="g_t")
+        hq = const.tile([P, 8, NB], U32, name="hq", align_bytes=64)
+        hs = const.tile([P, 8, NB], U8, name="hs", align_bytes=64)
+        wq = const.tile([P, 4, E], U32, name="wq", align_bytes=64)
+        ws = const.tile([P, 4, E], U8, name="ws", align_bytes=64)
+
+        xt = {}
+        wt = {}
+        EH = E // 2
+        for s in LOADS:
+            n = int(s[1:])
+            if s[0] == "x":
+                t = xpool.tile([P, E], BF16, name="xt")
+                if n == 0:
+                    nc.sync.dma_start(out=t[:, 0:EH], in_=x[0:P, 0:EH])
+                    nc.sync.dma_start(out=t[:, EH:E], in_=x[0:P, EH:E])
+                else:
+                    nc.sync.dma_start(out=t[:], in_=x[n * P:(n + 1) * P, :])
+                xt[n] = t
+            else:
+                for a in range(4):
+                    t = wpool.tile([P, E], BF16, name="wt")
+                    wt[(n, a)] = t
+                if n == 0:
+                    for half in range(2):
+                        for a in range(2):
+                            nc.sync.dma_start(out=wt[(0, a)][:, half * EH:(half + 1) * EH],
+                                              in_=W_in[a * P:(a + 1) * P, half * EH:(half + 1) * EH])
+                for a in range(4):
+                    if n > 0 or a >= 2:
+                        r0 = n * NB + a * P
+                        nc.sync.dma_start(out=wt[(n, a)][:], in_=W_in[r0:r0 + P, :])
+
+        gps = tps.tile([P, 2, P], F32, name="gps", tag="tp")
+        for u in range(2):
+            nc.tensor.transpose(gps[:, u, :], graw[:].bitcast(F32)[:, u:NH:2], ident[:])
+        for u in range(2):
+            nc.vector.tensor_copy(out=g_t[:].rearrange("p (c u e) -> p u c e", u=2, e=2)[:, u, :, :],
+                                  in_=gps[:, u, 0:4].bitcast(BF16).rearrange("p (c e) -> p c e", e=2))
+
+        st = {}
+
+        def stats(i):
+            ss = small.tile([P, 1], F32, name="ss")
+            rms = small.tile([P, 1], F32, name="rms")
+            if i == 0:
+                nc.scalar.activation(out=junk[:, 0:EH], in_=xt[i][:, 0:EH], func=ACT.Square, accum_out=ss[:])
+                ss2 = const.tile([P, 1], F32, name="ss2")
+                nc.scalar.activation(out=junk[:, EH:E], in_=xt[i][:, EH:E], func=ACT.Square, accum_out=ss2[:])
+                part = const.tile([P, 1], F32, name="part")
+                nc.scalar.activation(out=part[:], in_=ss2[:], func=ACT.Identity, bias=eps[:], scale=1.0 / E)
+                nc.scalar.activation(out=rms[:], in_=ss[:], func=ACT.Sqrt, bias=part[:], scale=1.0 / E)
+            else:
+                nc.scalar.activation(out=junk[:], in_=xt[i][:], func=ACT.Square, accum_out=ss[:])
+                nc.scalar.activation(out=rms[:], in_=ss[:], func=ACT.Sqrt, bias=eps[:], scale=1.0 / E)
+            st[("rms", i)] = rms
+
+        def scale(i):
+            rstd = small.tile([P, 1], F32, name="rstd")
+            nc.vector.reciprocal(out=rstd[:], in_=st[("rms", i)][:])
+            z = zpool.tile([P, E], F32, name="z")
+            nc.vector.tensor_scalar(
+                out=z[:].rearrange("p (c t j) -> p c t j", c=4, t=4),
+                in0=xt[i][:].rearrange("p (c j t) -> p c t j", c=4, t=4),
+                scalar1=rstd[:, 0:1], scalar2=None, op0=ALU.mult)
+            st[("z", i)] = z
+
+        def trx(i):
+            z = st[("z", i)]
+            banks = []
+            for c in range(4):
+                bank = tps.tile([P, 4, P], F32, name="xbank", tag="tp")
+                for t in range(4):
+                    col = (4 * c + t) * P
+                    nc.tensor.transpose(bank[:, t, :], z[:, col:col + P], ident[:])
+                banks.append(bank)
+            st[("xb", i)] = banks
+
+        def outx(i):
+            gh = ghpool.tile([P, 4, P, 4], BF16, name="gh", align_bytes=64)
+            for c in range(4):
+                nc.vector.tensor_tensor(
+                    out=gh[:, c, :, :], in0=st[("xb", i)][c][:].rearrange("p t r -> p r t"),
+                    in1=g_t[:, 4 * c:4 * c + 4].unsqueeze(1).to_broadcast([P, P, 4]), op=ALU.mult)
+            st[("gh", i)] = gh
+
+        def qx(i):
+            nc.vector.quantize_mx(out=hq[:, i, :].bitcast(FP8X4), scales=hs[:, i, :],
+                                  in_=st[("gh", i)][:].rearrange("p c r t -> p (c r t)"))
+
+        def trw(j, h):
+            banks = []
+            for c in range(4):
+                bank = tps.tile([P, 2, NH], F32, name="wbank", tag="tp")
+                for u in range(2):
+                    for a in range(2):
+                        w0 = c * NH + u
+                        nc.tensor.transpose(bank[:, u, a * P:(a + 1) * P],
+                                            wt[(j, 2 * h + a)][:].bitcast(F32)[:, w0:(c + 1) * NH:2], ident[:])
+                banks.append(bank)
+            st[("wb", j, h)] = banks
+
+        def outw(j, h, engines):
+            gw = gwpool.tile([P, 4, 4 * NH], BF16, name="gw", align_bytes=64)
+            for c in range(4):
+                dst = gw[:, c, :].bitcast(F32).rearrange("p (n u) -> p n u", u=2)
+                src = st[("wb", j, h)][c][:].rearrange("p u n -> p n u")
+                if engines[c] == "S":
+                    nc.scalar.copy(out=dst, in_=src)
+                else:
+                    nc.vector.tensor_copy(out=dst, in_=src)
+            st[("gw", j, h)] = gw
+
+        def qw(j, h):
+            n0 = j * NB + h * NH
+            for c in range(4):
+                nc.vector.quantize_mx(out=wq[:, c, n0:n0 + NH].bitcast(FP8X4), scales=ws[:, c, n0:n0 + NH],
+                                      in_=st[("gw", j, h)][:, c, :])
+
+        def mm(i, j):
+            acc = accs.tile([P, NB], F32, name="acc")
+            for c in range(4):
+                nc.tensor.matmul_mx(
+                    out=acc[:],
+                    lhsT=hq[:, i, c * P:(c + 1) * P].bitcast(FP8X4), lhsT_scale=hs[:, i, c * P:(c + 1) * P],
+                    rhs=wq[:, c, j * NB:(j + 1) * NB].bitcast(FP8X4), rhs_scale=ws[:, c, j * NB:(j + 1) * NB],
+                    start=(c == 0), stop=(c == 3))
+            st[("acc", i, j)] = acc
+
+        def outc(i, j, engine):
+            res = respool.tile([P, NB], F32, name="res")
+            if engine == "S":
+                nc.scalar.copy(out=res[:], in_=st[("acc", i, j)][:])
+            else:
+                nc.vector.tensor_copy(out=res[:], in_=st[("acc", i, j)][:])
+            nc.sync.dma_start(out=o[i * P:(i + 1) * P, j * NB:(j + 1) * NB], in_=res[:])
+
+        stats(0)
+        trw(0, 0)
+        scale(0)
+        outw(0, 0, "SSSS")
+        trx(0)
+        stats(1)
+        qw(0, 0)
+        outx(0)
+        trw(0, 1)
+        scale(1)
+        qx(0)
+        outw(0, 1, "SSSS")
+        trx(1)
+        stats(2)
+        outx(1)
+        trw(1, 0)
+        qw(0, 1)
+        qx(1)
+        mm(0, 0)
+        outw(1, 0, "SSSS")
+        scale(2)
+        outc(0, 0, "S")
+        units = ((1, 1), (2, 0), (2, 1), (3, 0), (3, 1))
+        cells = ((1, 0), (0, 1), (1, 1), (0, 2), (1, 2))
+        prev = (1, 0)
+        for n in range(5):
+            trw(units[n][0], units[n][1])
+            qw(prev[0], prev[1])
+            mm(cells[n][0], cells[n][1])
+            outw(units[n][0], units[n][1], "VSVS")
+            if n == 0:
+                stats(3)
+            if n == 4:
+                stats(4)
+                stats(5)
+            outc(cells[n][0], cells[n][1], "S")
+            prev = units[n]
+        trx(2)
+        qw(3, 1)
+        scale(3)
+        outx(2)
+        mm(0, 3)
+        mm(1, 3)
+        qx(2)
+        outc(0, 3, "S")
+        outc(1, 3, "S")
+        stats(6)
+        for i in range(3, 8):
+            trx(i)
+            if i < 7:
+                scale(i + 1)
+            outx(i)
+            for j in range(4):
+                mm(i - 1, j)
+            qx(i)
+            for j in range(4):
+                outc(i - 1, j, "S")
+            if i == 3:
+                stats(7)
+        for j in range(3):
+            mm(7, j)
+        halves = []
+        for h in range(2):
+            acc = accs.tile([P, NH], F32, name="acch", tag="acc")
+            n0 = 3 * NB + h * NH
+            for c in range(4):
+                nc.tensor.matmul_mx(
+                    out=acc[:],
+                    lhsT=hq[:, 7, c * P:(c + 1) * P].bitcast(FP8X4), lhsT_scale=hs[:, 7, c * P:(c + 1) * P],
+                    rhs=wq[:, c, n0:n0 + NH].bitcast(FP8X4), rhs_scale=ws[:, c, n0:n0 + NH],
+                    start=(c == 0), stop=(c == 3))
+            halves.append(acc)
+        for j in range(3):
+            outc(7, j, "V" if j % 2 else "S")
+        for h in range(2):
+            res = respool.tile([P, NH], F32, name="resh", tag="res")
+            if h == 0:
+                nc.vector.tensor_copy(out=res[:], in_=halves[h][:])
+            else:
+                nc.scalar.copy(out=res[:], in_=halves[h][:])
+            n0 = 3 * NB + h * NH
+            nc.sync.dma_start(out=o[7 * P:8 * P, n0:n0 + NH], in_=res[:])

@@ -14,12 +14,13 @@ ALU = mybir.AluOpType
 P = 128
 R = 1024
 E = 2048
+EH = E // 2
 NB = 512
 NH = 256
 EPS = 1e-6
 FLOPS = 2 * R * E * E
 
-LOADS = ("x0", "w0", "x1", "w1", "x2", "x3", "w2", "w3", "x4", "x5", "x6", "x7")
+LOADS = ("x0", "w0", "w1", "x1", "w2", "w3", "x2", "x3", "x4", "x5", "x6", "x7")
 
 
 def tile_hopfieldmemorylayer_pa_kernel(tc, query_input, norm_query_w, W_in, out):
@@ -30,26 +31,27 @@ def tile_hopfieldmemorylayer_pa_kernel(tc, query_input, norm_query_w, W_in, out)
         const = ctx.enter_context(tc.tile_pool(name="const", bufs=1))
         xpool = ctx.enter_context(tc.tile_pool(name="xpool", bufs=8))
         wpool = ctx.enter_context(tc.tile_pool(name="wpool", bufs=16))
-        zpool = ctx.enter_context(tc.tile_pool(name="zpool", bufs=2))
+        hpool = ctx.enter_context(tc.tile_pool(name="hpool", bufs=2))
         small = ctx.enter_context(tc.tile_pool(name="small", bufs=8))
         ghpool = ctx.enter_context(tc.tile_pool(name="ghpool", bufs=2))
-        gwpool = ctx.enter_context(tc.tile_pool(name="gwpool", bufs=2))
+        gwpool = ctx.enter_context(tc.tile_pool(name="gwpool", bufs=3))
         respool = ctx.enter_context(tc.tile_pool(name="respool", bufs=8))
         tps = ctx.enter_context(tc.psum_pool(name="tps", bufs=4))
         accs = ctx.enter_context(tc.psum_pool(name="accs", bufs=4))
         ctx.enter_context(tc.manual_schedule())
 
+        graw = const.tile([P, NB], BF16, name="graw")
+        nc.vector.memset(graw[:], 0.0)
+        identb = const.tile([P, P], BF16, name="identb")
+        make_identity(nc, identb[:])
         ident = const.tile([P, P], F32, name="ident")
         make_identity(nc, ident[:])
         eps = const.tile([P, 1], F32, name="eps")
         nc.vector.memset(eps[:], EPS)
         warm = const.tile([P, 1], F32, name="warm")
         nc.scalar.activation(out=warm[:], in_=eps[:], func=ACT.Sqrt)
-        graw = const.tile([P, NB], BF16, name="graw")
-        nc.vector.memset(graw[:], 0.0)
-        nc.sync.dma_start(out=graw[0:4, :], in_=norm_query_w.rearrange("(c w) -> c w", w=NB))
         junk = const.tile([P, E], BF16, name="junk")
-        g_t = const.tile([P, 16], F32, name="g_t")
+        gb = const.tile([P, E], BF16, name="gb")
         hq = const.tile([P, 8, NB], U32, name="hq", align_bytes=64)
         hs = const.tile([P, 8, NB], U8, name="hs", align_bytes=64)
         wq = const.tile([P, 4, E], U32, name="wq", align_bytes=64)
@@ -57,13 +59,13 @@ def tile_hopfieldmemorylayer_pa_kernel(tc, query_input, norm_query_w, W_in, out)
 
         xt = {}
         wt = {}
-        EH = E // 2
         for s in LOADS:
             n = int(s[1:])
             if s[0] == "x":
                 t = xpool.tile([P, E], BF16, name="xt")
                 if n == 0:
                     nc.sync.dma_start(out=t[:, 0:EH], in_=x[0:P, 0:EH])
+                    nc.sync.dma_start(out=graw[0:4, :], in_=norm_query_w.rearrange("(c w) -> c w", w=NB))
                     nc.sync.dma_start(out=t[:, EH:E], in_=x[0:P, EH:E])
                 else:
                     nc.sync.dma_start(out=t[:], in_=x[n * P:(n + 1) * P, :])
@@ -82,14 +84,14 @@ def tile_hopfieldmemorylayer_pa_kernel(tc, query_input, norm_query_w, W_in, out)
                         r0 = n * NB + a * P
                         nc.sync.dma_start(out=wt[(n, a)][:], in_=W_in[r0:r0 + P, :])
 
-        gps = tps.tile([P, 2, P], F32, name="gps", tag="tp")
-        for u in range(2):
-            nc.tensor.transpose(gps[:, u, :], graw[:].bitcast(F32)[:, u:NH:2], ident[:])
-        for u in range(2):
-            nc.vector.tensor_copy(out=g_t[:].rearrange("p (c u e) -> p u c e", u=2, e=2)[:, u, :, :],
-                                  in_=gps[:, u, 0:4].bitcast(BF16).rearrange("p (c e) -> p c e", e=2))
-
         st = {}
+
+        def gain():
+            for c in range(4):
+                gps = tps.tile([P, NB], F32, name="gps", tag="tp")
+                nc.tensor.matmul(gps[:], lhsT=identb[:, c:c + 1].to_broadcast([P, P]), rhs=graw[:], start=True, stop=True)
+                nc.vector.tensor_copy(out=gb[:].rearrange("p (u c j e) -> p c u j e", u=2, c=4, e=2)[:, c],
+                                      in_=gps[:].rearrange("p (j u e) -> p u j e", u=2, e=2))
 
         def stats(i):
             ss = small.tile([P, 1], F32, name="ss")
@@ -106,38 +108,48 @@ def tile_hopfieldmemorylayer_pa_kernel(tc, query_input, norm_query_w, W_in, out)
                 nc.scalar.activation(out=rms[:], in_=ss[:], func=ACT.Sqrt, bias=eps[:], scale=1.0 / E)
             st[("rms", i)] = rms
 
-        def scale(i):
+        def recip(i):
             rstd = small.tile([P, 1], F32, name="rstd")
             nc.vector.reciprocal(out=rstd[:], in_=st[("rms", i)][:])
-            z = zpool.tile([P, E], F32, name="z")
-            nc.vector.tensor_scalar(
-                out=z[:].rearrange("p (c t j) -> p c t j", c=4, t=4),
-                in0=xt[i][:].rearrange("p (c j t) -> p c t j", c=4, t=4),
-                scalar1=rstd[:, 0:1], scalar2=None, op0=ALU.mult)
-            st[("z", i)] = z
+            st[("rstd", i)] = rstd
+            h = hpool.tile([P, E], BF16, name="h")
+            st[("h", i)] = h
+
+        def scale(i, u):
+            h = st[("h", i)]
+            nc.vector.scalar_tensor_tensor(
+                out=h[:, u * EH:(u + 1) * EH].rearrange("p (q e) -> p q e", e=2),
+                in0=xt[i][:].rearrange("p (q u e) -> p u q e", u=2, e=2)[:, u],
+                scalar=st[("rstd", i)][:, 0:1],
+                in1=gb[:, u * EH:(u + 1) * EH].rearrange("p (q e) -> p q e", e=2),
+                op0=ALU.mult, op1=ALU.mult)
 
         def trx(i):
-            z = st[("z", i)]
+            words = st[("h", i)][:].bitcast(F32)
             banks = []
-            for c in range(4):
-                bank = tps.tile([P, 4, P], F32, name="xbank", tag="tp")
-                for t in range(4):
-                    col = (4 * c + t) * P
-                    nc.tensor.transpose(bank[:, t, :], z[:, col:col + P], ident[:])
+            for k in range(2):
+                bank = tps.tile([P, 2, 2, P], F32, name="xbank", tag="tp")
                 banks.append(bank)
+            for u in range(2):
+                for k in range(2):
+                    for v in range(2):
+                        col = u * NB + (2 * k + v) * P
+                        nc.tensor.transpose(banks[k][:, v, u, :], words[:, col:col + P], ident[:])
             st[("xb", i)] = banks
+            st[("gh", i)] = ghpool.tile([P, 4, 4 * P], BF16, name="gh", align_bytes=64)
 
-        def outx(i):
-            gh = ghpool.tile([P, 4, P, 4], BF16, name="gh", align_bytes=64)
-            for c in range(4):
-                nc.vector.tensor_tensor(
-                    out=gh[:, c, :, :], in0=st[("xb", i)][c][:].rearrange("p t r -> p r t"),
-                    in1=g_t[:, 4 * c:4 * c + 4].unsqueeze(1).to_broadcast([P, P, 4]), op=ALU.mult)
-            st[("gh", i)] = gh
+        def outx(i, k, engine):
+            gh = st[("gh", i)]
+            dst = gh[:, 2 * k:2 * k + 2, :].bitcast(F32).rearrange("p c (r u) -> p c r u", u=2)
+            src = st[("xb", i)][k][:].rearrange("p c u r -> p c r u")
+            if engine == "S":
+                nc.scalar.copy(out=dst, in_=src)
+            else:
+                nc.vector.tensor_copy(out=dst, in_=src)
 
         def qx(i):
             nc.vector.quantize_mx(out=hq[:, i, :].bitcast(FP8X4), scales=hs[:, i, :],
-                                  in_=st[("gh", i)][:].rearrange("p c r t -> p (c r t)"))
+                                  in_=st[("gh", i)][:].rearrange("p c w -> p (c w)"))
 
         def trw(j, h):
             banks = []
@@ -151,20 +163,21 @@ def tile_hopfieldmemorylayer_pa_kernel(tc, query_input, norm_query_w, W_in, out)
                 banks.append(bank)
             st[("wb", j, h)] = banks
 
-        def outw(j, h, engines):
-            gw = gwpool.tile([P, 4, 4 * NH], BF16, name="gw", align_bytes=64)
-            for c in range(4):
+        def outw(j, h, engines, cs=(0, 1, 2, 3)):
+            if cs[0] == 0:
+                st[("gw", j, h)] = gwpool.tile([P, 4, 4 * NH], BF16, name="gw", align_bytes=64)
+            gw = st[("gw", j, h)]
+            for c in cs:
                 dst = gw[:, c, :].bitcast(F32).rearrange("p (n u) -> p n u", u=2)
                 src = st[("wb", j, h)][c][:].rearrange("p u n -> p n u")
                 if engines[c] == "S":
                     nc.scalar.copy(out=dst, in_=src)
                 else:
                     nc.vector.tensor_copy(out=dst, in_=src)
-            st[("gw", j, h)] = gw
 
-        def qw(j, h):
+        def qw(j, h, cs=(0, 1, 2, 3)):
             n0 = j * NB + h * NH
-            for c in range(4):
+            for c in cs:
                 nc.vector.quantize_mx(out=wq[:, c, n0:n0 + NH].bitcast(FP8X4), scales=ws[:, c, n0:n0 + NH],
                                       in_=st[("gw", j, h)][:, c, :])
 
@@ -186,65 +199,95 @@ def tile_hopfieldmemorylayer_pa_kernel(tc, query_input, norm_query_w, W_in, out)
                 nc.vector.tensor_copy(out=res[:], in_=st[("acc", i, j)][:])
             nc.sync.dma_start(out=o[i * P:(i + 1) * P, j * NB:(j + 1) * NB], in_=res[:])
 
+        gain()
         stats(0)
         trw(0, 0)
-        scale(0)
         outw(0, 0, "SSSS")
-        trx(0)
-        stats(1)
-        qw(0, 0)
-        outx(0)
+        recip(0)
+        scale(0, 0)
+        scale(0, 1)
         trw(0, 1)
-        scale(1)
-        qx(0)
-        outw(0, 1, "SSSS")
-        trx(1)
-        stats(2)
-        outx(1)
-        trw(1, 0)
+        qw(0, 0)
+        outw(0, 1, "SSVS")
+        trx(0)
+        outx(0, 0, "S")
         qw(0, 1)
-        qx(1)
+        trw(1, 0)
+        outx(0, 1, "S")
+        outw(1, 0, "VSSV", (0, 1))
+        qx(0)
+        outw(1, 0, "VSSV", (2, 3))
+        stats(1)
+        trw(1, 1)
+        qw(1, 0)
+        outw(1, 1, "VVSV")
+        trw(2, 0)
+        qw(1, 1)
+        outw(2, 0, "SSSV")
+        trw(2, 1)
+        qw(2, 0)
+        outw(2, 1, "SSSV")
         mm(0, 0)
-        outw(1, 0, "SSSS")
-        scale(2)
+        recip(1)
+        qw(2, 1)
+        scale(1, 0)
+        scale(1, 1)
         outc(0, 0, "S")
-        units = ((1, 1), (2, 0), (2, 1), (3, 0), (3, 1))
-        cells = ((1, 0), (0, 1), (1, 1), (0, 2), (1, 2))
-        prev = (1, 0)
-        for n in range(5):
-            trw(units[n][0], units[n][1])
-            qw(prev[0], prev[1])
-            mm(cells[n][0], cells[n][1])
-            outw(units[n][0], units[n][1], "VSVS")
-            if n == 0:
-                stats(3)
-            if n == 4:
-                stats(4)
-                stats(5)
-            outc(cells[n][0], cells[n][1], "S")
-            prev = units[n]
-        trx(2)
+        trw(3, 0)
+        outw(3, 0, "SSSV")
+        mm(0, 1)
+        stats(2)
+        trx(1)
+        qw(3, 0)
+        outc(0, 1, "V")
+        outx(1, 0, "V")
+        outx(1, 1, "S")
+        trw(3, 1)
+        outw(3, 1, "SVVV", (0, 1))
+        qx(1)
+        outw(3, 1, "SVVV", (2, 3))
+        mm(0, 2)
+        stats(3)
+        recip(2)
         qw(3, 1)
-        scale(3)
-        outx(2)
+        outc(0, 2, "S")
+        mm(1, 0)
+        mm(1, 1)
+        mm(1, 2)
+        scale(2, 0)
+        outc(1, 0, "V")
+        scale(2, 1)
+        outc(1, 1, "S")
+        stats(4)
+        recip(3)
+        outc(1, 2, "V")
+        trx(2)
         mm(0, 3)
         mm(1, 3)
+        scale(3, 0)
+        outx(2, 0, "V")
+        outx(2, 1, "V")
+        scale(3, 1)
         qx(2)
         outc(0, 3, "S")
         outc(1, 3, "S")
-        stats(6)
         for i in range(3, 8):
             trx(i)
+            outx(i, 0, "V")
+            outx(i, 1, "V")
             if i < 7:
-                scale(i + 1)
-            outx(i)
+                recip(i + 1)
+                scale(i + 1, 0)
+            qx(i)
+            if i < 7:
+                scale(i + 1, 1)
             for j in range(4):
                 mm(i - 1, j)
-            qx(i)
-            for j in range(4):
+            outc(i - 1, 0, "S")
+            if i < 6:
+                stats(i + 2)
+            for j in range(1, 4):
                 outc(i - 1, j, "S")
-            if i == 3:
-                stats(7)
         for j in range(3):
             mm(7, j)
         halves = []

@@ -36,8 +36,7 @@ def tile_hopfieldmemorylayer_pa_kernel(tc, query_input, norm_query_w, W_in, out)
         ghpool = ctx.enter_context(tc.tile_pool(name="ghpool", bufs=2))
         gwpool = ctx.enter_context(tc.tile_pool(name="gwpool", bufs=3))
         respool = ctx.enter_context(tc.tile_pool(name="respool", bufs=8))
-        tps = ctx.enter_context(tc.psum_pool(name="tps", bufs=4))
-        accs = ctx.enter_context(tc.psum_pool(name="accs", bufs=4))
+        psum = ctx.enter_context(tc.psum_pool(name="psum", bufs=8))
         ctx.enter_context(tc.manual_schedule())
 
         graw = const.tile([P, NB], BF16, name="graw")
@@ -88,7 +87,7 @@ def tile_hopfieldmemorylayer_pa_kernel(tc, query_input, norm_query_w, W_in, out)
 
         def gain():
             for c in range(4):
-                gps = tps.tile([P, NB], F32, name="gps", tag="tp")
+                gps = psum.tile([P, NB], F32, name="gps", tag="ps")
                 nc.tensor.matmul(gps[:], lhsT=identb[:, c:c + 1].to_broadcast([P, P]), rhs=graw[:], start=True, stop=True)
                 nc.vector.tensor_copy(out=gb[:].rearrange("p (u c j e) -> p c u j e", u=2, c=4, e=2)[:, c],
                                       in_=gps[:].rearrange("p (j u e) -> p u j e", u=2, e=2))
@@ -128,7 +127,7 @@ def tile_hopfieldmemorylayer_pa_kernel(tc, query_input, norm_query_w, W_in, out)
             words = st[("h", i)][:].bitcast(F32)
             banks = []
             for k in range(2):
-                bank = tps.tile([P, 2, 2, P], F32, name="xbank", tag="tp")
+                bank = psum.tile([P, 2, 2, P], F32, name="xbank", tag="ps")
                 banks.append(bank)
             for u in range(2):
                 for k in range(2):
@@ -154,7 +153,7 @@ def tile_hopfieldmemorylayer_pa_kernel(tc, query_input, norm_query_w, W_in, out)
         def trw(j, h):
             banks = []
             for c in range(4):
-                bank = tps.tile([P, 2, NH], F32, name="wbank", tag="tp")
+                bank = psum.tile([P, 2, NH], F32, name="wbank", tag="ps")
                 for u in range(2):
                     for a in range(2):
                         w0 = c * NH + u
@@ -182,7 +181,7 @@ def tile_hopfieldmemorylayer_pa_kernel(tc, query_input, norm_query_w, W_in, out)
                                       in_=st[("gw", j, h)][:, c, :])
 
         def mm(i, j):
-            acc = accs.tile([P, NB], F32, name="acc")
+            acc = psum.tile([P, NB], F32, name="acc", tag="ps")
             for c in range(4):
                 nc.tensor.matmul_mx(
                     out=acc[:],
@@ -265,7 +264,7 @@ def tile_hopfieldmemorylayer_pa_kernel(tc, query_input, norm_query_w, W_in, out)
         mm(0, 3)
         mm(1, 3)
         scale(3, 0)
-        outx(2, 0, "V")
+        outx(2, 0, "S")
         outx(2, 1, "V")
         scale(3, 1)
         qx(2)
@@ -273,7 +272,7 @@ def tile_hopfieldmemorylayer_pa_kernel(tc, query_input, norm_query_w, W_in, out)
         outc(1, 3, "S")
         for i in range(3, 8):
             trx(i)
-            outx(i, 0, "V")
+            outx(i, 0, "S")
             outx(i, 1, "V")
             if i < 7:
                 recip(i + 1)
@@ -286,13 +285,14 @@ def tile_hopfieldmemorylayer_pa_kernel(tc, query_input, norm_query_w, W_in, out)
             outc(i - 1, 0, "S")
             if i < 6:
                 stats(i + 2)
-            for j in range(1, 4):
-                outc(i - 1, j, "S")
+            outc(i - 1, 1, "S")
+            outc(i - 1, 2, "S")
+            outc(i - 1, 3, "V")
         for j in range(3):
             mm(7, j)
         halves = []
         for h in range(2):
-            acc = accs.tile([P, NH], F32, name="acch", tag="acc")
+            acc = psum.tile([P, NH], F32, name="acch", tag="ps")
             n0 = 3 * NB + h * NH
             for c in range(4):
                 nc.tensor.matmul_mx(

@@ -48,7 +48,7 @@ def tile_hopfieldmemorylayer_pa_kernel(tc, query_input, norm_query_w, W_in, out)
         eps = const.tile([P, 1], F32, name="eps")
         nc.vector.memset(eps[:], EPS)
         warm = const.tile([P, 1], F32, name="warm")
-        nc.scalar.activation(out=warm[:], in_=eps[:], func=ACT.Sqrt)
+        nc.scalar.activation(out=warm[:], in_=eps[:], func=ACT.Abs_reciprocal_sqrt)
         junk = const.tile([P, E], BF16, name="junk")
         gb = const.tile([P, E], BF16, name="gb")
         hq = const.tile([P, 8, NB], U32, name="hq", align_bytes=64)
@@ -101,16 +101,13 @@ def tile_hopfieldmemorylayer_pa_kernel(tc, query_input, norm_query_w, W_in, out)
                 nc.scalar.activation(out=junk[:, EH:E], in_=xt[i][:, EH:E], func=ACT.Square, accum_out=ss2[:])
                 part = const.tile([P, 1], F32, name="part")
                 nc.scalar.activation(out=part[:], in_=ss2[:], func=ACT.Identity, bias=eps[:], scale=1.0 / E)
-                nc.scalar.activation(out=rms[:], in_=ss[:], func=ACT.Sqrt, bias=part[:], scale=1.0 / E)
+                nc.scalar.activation(out=rms[:], in_=ss[:], func=ACT.Abs_reciprocal_sqrt, bias=part[:], scale=1.0 / E)
             else:
                 nc.scalar.activation(out=junk[:], in_=xt[i][:], func=ACT.Square, accum_out=ss[:])
-                nc.scalar.activation(out=rms[:], in_=ss[:], func=ACT.Sqrt, bias=eps[:], scale=1.0 / E)
-            st[("rms", i)] = rms
+                nc.scalar.activation(out=rms[:], in_=ss[:], func=ACT.Abs_reciprocal_sqrt, bias=eps[:], scale=1.0 / E)
+            st[("rstd", i)] = rms
 
         def recip(i):
-            rstd = small.tile([P, 1], F32, name="rstd")
-            nc.vector.reciprocal(out=rstd[:], in_=st[("rms", i)][:])
-            st[("rstd", i)] = rstd
             h = hpool.tile([P, E], BF16, name="h")
             st[("h", i)] = h
 
@@ -206,88 +203,61 @@ def tile_hopfieldmemorylayer_pa_kernel(tc, query_input, norm_query_w, W_in, out)
         scale(0, 0)
         scale(0, 1)
         trw(0, 1)
+        outw(0, 1, "SSSS")
         qw(0, 0)
-        outw(0, 1, "SSVS")
         trx(0)
         outx(0, 0, "S")
-        qw(0, 1)
-        trw(1, 0)
         outx(0, 1, "S")
+        trw(1, 0)
         outw(1, 0, "VSSV", (0, 1))
+        qw(0, 1)
         qx(0)
         outw(1, 0, "VSSV", (2, 3))
-        stats(1)
         trw(1, 1)
+        outw(1, 1, "SSSV")
         qw(1, 0)
-        outw(1, 1, "VVSV")
+        stats(1)
         trw(2, 0)
+        outw(2, 0, "VVSV")
         qw(1, 1)
-        outw(2, 0, "SSSV")
         trw(2, 1)
-        qw(2, 0)
         outw(2, 1, "SSSV")
-        mm(0, 0)
-        recip(1)
-        qw(2, 1)
-        scale(1, 0)
-        scale(1, 1)
-        outc(0, 0, "S")
+        qw(2, 0)
         trw(3, 0)
         outw(3, 0, "SSSV")
-        mm(0, 1)
-        stats(2)
-        trx(1)
-        qw(3, 0)
-        outc(0, 1, "V")
-        outx(1, 0, "V")
-        outx(1, 1, "S")
+        recip(1)
+        scale(1, 0)
+        qw(2, 1)
         trw(3, 1)
-        outw(3, 1, "SVVV", (0, 1))
-        qx(1)
-        outw(3, 1, "SVVV", (2, 3))
-        mm(0, 2)
-        stats(3)
-        recip(2)
+        outw(3, 1, "SSSS")
+        scale(1, 1)
+        qw(3, 0)
         qw(3, 1)
-        outc(0, 2, "S")
-        mm(1, 0)
-        mm(1, 1)
-        mm(1, 2)
-        scale(2, 0)
-        outc(1, 0, "V")
-        scale(2, 1)
-        outc(1, 1, "S")
-        stats(4)
-        recip(3)
-        outc(1, 2, "V")
-        trx(2)
-        mm(0, 3)
-        mm(1, 3)
-        scale(3, 0)
-        outx(2, 0, "S")
-        outx(2, 1, "V")
-        scale(3, 1)
-        qx(2)
-        outc(0, 3, "S")
-        outc(1, 3, "S")
-        for i in range(3, 8):
+        stats(2)
+        for i in range(1, 8):
+            mm(i - 1, 0)
             trx(i)
-            outx(i, 0, "S")
-            outx(i, 1, "V")
-            if i < 7:
+            for j in range(1, 4):
+                mm(i - 1, j)
+            if i > 1:
+                outc(i - 2, 3, "V")
+            outc(i - 1, 0, "S")
+            if 1 < i < 7:
                 recip(i + 1)
                 scale(i + 1, 0)
+            outx(i, 0, "S")
+            outx(i, 1, "V")
             qx(i)
+            if i == 1:
+                recip(i + 1)
+                scale(i + 1, 0)
             if i < 7:
                 scale(i + 1, 1)
-            for j in range(4):
-                mm(i - 1, j)
-            outc(i - 1, 0, "S")
             if i < 6:
                 stats(i + 2)
             outc(i - 1, 1, "S")
             outc(i - 1, 2, "S")
-            outc(i - 1, 3, "V")
+        outc(6, 3, "V")
         for j in range(3):
             mm(7, j)
         halves = []

@@ -45,9 +45,9 @@ def tile_hopfieldmemorylayer_pa_kernel(tc, query_input, norm_query_w, W_in, out)
         make_identity(nc, identb[:])
         ident = const.tile([P, P], F32, name="ident")
         make_identity(nc, ident[:])
-        eps = const.tile([P, 1], F32, name="eps")
+        eps = const.tile([P, 16], F32, name="eps")
         nc.vector.memset(eps[:], EPS)
-        warm = const.tile([P, 1], F32, name="warm")
+        warm = const.tile([P, 16], F32, name="warm")
         nc.scalar.activation(out=warm[:], in_=eps[:], func=ACT.Abs_reciprocal_sqrt)
         junk = const.tile([P, E], BF16, name="junk")
         gb = const.tile([P, E], BF16, name="gb")
@@ -100,11 +100,11 @@ def tile_hopfieldmemorylayer_pa_kernel(tc, query_input, norm_query_w, W_in, out)
                 ss2 = const.tile([P, 1], F32, name="ss2")
                 nc.scalar.activation(out=junk[:, EH:E], in_=xt[i][:, EH:E], func=ACT.Square, accum_out=ss2[:])
                 part = const.tile([P, 1], F32, name="part")
-                nc.scalar.activation(out=part[:], in_=ss2[:], func=ACT.Identity, bias=eps[:], scale=1.0 / E)
+                nc.scalar.activation(out=part[:], in_=ss2[:], func=ACT.Identity, bias=eps[:, 0:1], scale=1.0 / E)
                 nc.scalar.activation(out=rms[:], in_=ss[:], func=ACT.Abs_reciprocal_sqrt, bias=part[:], scale=1.0 / E)
             else:
                 nc.scalar.activation(out=junk[:], in_=xt[i][:], func=ACT.Square, accum_out=ss[:])
-                nc.scalar.activation(out=rms[:], in_=ss[:], func=ACT.Abs_reciprocal_sqrt, bias=eps[:], scale=1.0 / E)
+                nc.scalar.activation(out=rms[:], in_=ss[:], func=ACT.Abs_reciprocal_sqrt, bias=eps[:, 0:1], scale=1.0 / E)
             st[("rstd", i)] = rms
 
         def recip(i):

@@ -214,48 +214,71 @@ def tile_hopfieldmemorylayer_pa_kernel(tc, query_input, norm_query_w, W_in, out)
         qx(0)
         outw(1, 0, "VSSV", (2, 3))
         trw(1, 1)
+        mm(0, 0)
         outw(1, 1, "SSSV")
         qw(1, 0)
         stats(1)
+        outc(0, 0, "S")
         trw(2, 0)
-        outw(2, 0, "VVSV")
+        outw(2, 0, "VSVS")
         qw(1, 1)
+        recip(1)
+        scale(1, 0)
         trw(2, 1)
         outw(2, 1, "SSSV")
+        scale(1, 1)
         qw(2, 0)
         trw(3, 0)
         outw(3, 0, "SSSV")
-        recip(1)
-        scale(1, 0)
+        trx(1)
+        outx(1, 0, "S")
+        outx(1, 1, "V")
         qw(2, 1)
+        qx(1)
         trw(3, 1)
-        outw(3, 1, "SSSS")
-        scale(1, 1)
+        outw(3, 1, "SSSV")
         qw(3, 0)
-        qw(3, 1)
+        mm(0, 1)
+        mm(0, 2)
         stats(2)
-        for i in range(1, 8):
-            mm(i - 1, 0)
-            trx(i)
-            for j in range(1, 4):
+        qw(3, 1)
+        outc(0, 1, "S")
+        mm(1, 0)
+        mm(1, 1)
+        recip(2)
+        scale(2, 0)
+        outc(0, 2, "S")
+        scale(2, 1)
+        stats(3)
+        mm(0, 3)
+        outc(1, 0, "S")
+        recip(3)
+        scale(3, 0)
+        outc(1, 1, "S")
+        for i in range(2, 8):
+            lead = 0 if i == 2 else 1
+            for j in range(lead):
                 mm(i - 1, j)
-            if i > 1:
+            trx(i)
+            for j in range(2 if i == 2 else lead, 4):
+                mm(i - 1, j)
+            if i > 2:
                 outc(i - 2, 3, "V")
-            outc(i - 1, 0, "S")
-            if 1 < i < 7:
+                outc(i - 1, 0, "S")
+            if 2 < i < 7:
                 recip(i + 1)
                 scale(i + 1, 0)
             outx(i, 0, "S")
             outx(i, 1, "V")
             qx(i)
-            if i == 1:
-                recip(i + 1)
-                scale(i + 1, 0)
             if i < 7:
                 scale(i + 1, 1)
             if i < 6:
                 stats(i + 2)
-            outc(i - 1, 1, "S")
+            if i == 2:
+                outc(0, 3, "S")
+            else:
+                outc(i - 1, 1, "S")
             outc(i - 1, 2, "S")
         outc(6, 3, "V")
         for j in range(3):

@@ -187,6 +187,20 @@ def tile_hopfieldmemorylayer_pa_kernel(tc, query_input, norm_query_w, W_in, out)
                     start=(c == 0), stop=(c == 3))
             st[("acc", i, j)] = acc
 
+        def mm2(i, ja, jb):
+            accs = []
+            for j in (ja, jb):
+                acc = psum.tile([P, NB], F32, name="acc", tag="ps")
+                st[("acc", i, j)] = acc
+                accs.append(acc)
+            for c in range(4):
+                for acc, j in zip(accs, (ja, jb)):
+                    nc.tensor.matmul_mx(
+                        out=acc[:],
+                        lhsT=hq[:, i, c * P:(c + 1) * P].bitcast(FP8X4), lhsT_scale=hs[:, i, c * P:(c + 1) * P],
+                        rhs=wq[:, c, j * NB:(j + 1) * NB].bitcast(FP8X4), rhs_scale=ws[:, c, j * NB:(j + 1) * NB],
+                        start=(c == 0), stop=(c == 3))
+
         def outc(i, j, engine):
             res = respool.tile([P, NB], F32, name="res")
             if engine == "S":
@@ -238,13 +252,11 @@ def tile_hopfieldmemorylayer_pa_kernel(tc, query_input, norm_query_w, W_in, out)
         trw(3, 1)
         outw(3, 1, "SSSV")
         qw(3, 0)
-        mm(0, 1)
-        mm(0, 2)
+        mm2(0, 1, 2)
         stats(2)
         qw(3, 1)
         outc(0, 1, "S")
-        mm(1, 0)
-        mm(1, 1)
+        mm2(1, 0, 1)
         recip(2)
         scale(2, 0)
         outc(0, 2, "S")
@@ -256,12 +268,10 @@ def tile_hopfieldmemorylayer_pa_kernel(tc, query_input, norm_query_w, W_in, out)
         scale(3, 0)
         outc(1, 1, "S")
         for i in range(2, 8):
-            lead = 0 if i == 2 else 1
-            for j in range(lead):
-                mm(i - 1, j)
+            if i > 2:
+                mm2(i - 1, 0, 1)
             trx(i)
-            for j in range(2 if i == 2 else lead, 4):
-                mm(i - 1, j)
+            mm2(i - 1, 2, 3)
             if i > 2:
                 outc(i - 2, 3, "V")
                 outc(i - 1, 0, "S")

@@ -34,7 +34,7 @@ def tile_hopfieldmemorylayer_pa_kernel(tc, query_input, norm_query_w, W_in, out)
         hpool = ctx.enter_context(tc.tile_pool(name="hpool", bufs=2))
         small = ctx.enter_context(tc.tile_pool(name="small", bufs=8))
         ghpool = ctx.enter_context(tc.tile_pool(name="ghpool", bufs=2))
-        gwpool = ctx.enter_context(tc.tile_pool(name="gwpool", bufs=3))
+        gwpool = ctx.enter_context(tc.tile_pool(name="gwpool", bufs=4))
         respool = ctx.enter_context(tc.tile_pool(name="respool", bufs=8))
         psum = ctx.enter_context(tc.psum_pool(name="psum", bufs=8))
         ctx.enter_context(tc.manual_schedule())
@@ -87,7 +87,7 @@ def tile_hopfieldmemorylayer_pa_kernel(tc, query_input, norm_query_w, W_in, out)
 
         def gain():
             for c in range(4):
-                gps = psum.tile([P, NB], F32, name="gps", tag="ps")
+                gps = psum.tile([P, NB], BF16, name="gps", tag="ps")
                 nc.tensor.matmul(gps[:], lhsT=identb[:, c:c + 1].to_broadcast([P, P]), rhs=graw[:], start=True, stop=True)
                 nc.vector.tensor_copy(out=gb[:].rearrange("p (u c j e) -> p c u j e", u=2, c=4, e=2)[:, c],
                                       in_=gps[:].rearrange("p (j u e) -> p u j e", u=2, e=2))
@@ -151,12 +151,15 @@ def tile_hopfieldmemorylayer_pa_kernel(tc, query_input, norm_query_w, W_in, out)
             banks = []
             for c in range(4):
                 bank = psum.tile([P, 2, NH], F32, name="wbank", tag="ps")
-                for u in range(2):
-                    for a in range(2):
-                        w0 = c * NH + u
-                        nc.tensor.transpose(bank[:, u, a * P:(a + 1) * P],
-                                            wt[(j, 2 * h + a)][:].bitcast(F32)[:, w0:(c + 1) * NH:2], ident[:])
                 banks.append(bank)
+            runs = [(a, c) for a in range(2) for c in range(4)]
+            if (j, h) == (0, 0):
+                runs = [(a, c) for c in range(4) for a in range(2)]
+            for a, c in runs:
+                for u in range(2):
+                    w0 = c * NH + u
+                    nc.tensor.transpose(banks[c][:, u, a * P:(a + 1) * P],
+                                        wt[(j, 2 * h + a)][:].bitcast(F32)[:, w0:(c + 1) * NH:2], ident[:])
             st[("wb", j, h)] = banks
 
         def outw(j, h, engines, cs=(0, 1, 2, 3)):
@@ -220,7 +223,7 @@ def tile_hopfieldmemorylayer_pa_kernel(tc, query_input, norm_query_w, W_in, out)
         outw(0, 1, "SSSS")
         qw(0, 0)
         trx(0)
-        outx(0, 0, "S")
+        outx(0, 0, "V")
         outx(0, 1, "S")
         trw(1, 0)
         outw(1, 0, "VSSV", (0, 1))
@@ -229,18 +232,18 @@ def tile_hopfieldmemorylayer_pa_kernel(tc, query_input, norm_query_w, W_in, out)
         outw(1, 0, "VSSV", (2, 3))
         trw(1, 1)
         mm(0, 0)
-        outw(1, 1, "SSSV")
+        outw(1, 1, "SVSV")
         qw(1, 0)
         stats(1)
         outc(0, 0, "S")
         trw(2, 0)
         outw(2, 0, "VSVS")
-        qw(1, 1)
         recip(1)
         scale(1, 0)
-        trw(2, 1)
-        outw(2, 1, "SSSV")
         scale(1, 1)
+        qw(1, 1)
+        trw(2, 1)
+        outw(2, 1, "SSSS")
         qw(2, 0)
         trw(3, 0)
         outw(3, 0, "SSSV")
@@ -291,8 +294,8 @@ def tile_hopfieldmemorylayer_pa_kernel(tc, query_input, norm_query_w, W_in, out)
                 outc(i - 1, 1, "S")
             outc(i - 1, 2, "S")
         outc(6, 3, "V")
-        for j in range(3):
-            mm(7, j)
+        mm2(7, 0, 1)
+        mm(7, 2)
         halves = []
         for h in range(2):
             acc = psum.tile([P, NH], F32, name="acch", tag="ps")

from contextlib import ExitStack

import concourse.mybir as mybir
from concourse.masks import make_identity

F32 = mybir.dt.float32
BF16 = mybir.dt.bfloat16
U32 = mybir.dt.uint32
U8 = mybir.dt.uint8
FP8X4 = mybir.dt.float8_e4m3fn_x4
ACT = mybir.ActivationFunctionType
ALU = mybir.AluOpType

P = 128
R = 1024
E = 2048
EH = E // 2
NB = 512
NH = 256
EPS = 1e-6
FLOPS = 2 * R * E * E

LOADS = ("x0", "w0", "w1", "x1", "w2", "w3", "x2", "x3", "x4", "x5", "x6", "x7")


def tile_hopfieldmemorylayer_pa_kernel(tc, query_input, norm_query_w, W_in, out):
    nc = tc.nc
    x = query_input.flatten_outer_dims()
    o = out.flatten_outer_dims()
    with ExitStack() as ctx:
        const = ctx.enter_context(tc.tile_pool(name="const", bufs=1))
        xpool = ctx.enter_context(tc.tile_pool(name="xpool", bufs=8))
        wpool = ctx.enter_context(tc.tile_pool(name="wpool", bufs=16))
        hpool = ctx.enter_context(tc.tile_pool(name="hpool", bufs=2))
        small = ctx.enter_context(tc.tile_pool(name="small", bufs=8))
        ghpool = ctx.enter_context(tc.tile_pool(name="ghpool", bufs=2))
        gwpool = ctx.enter_context(tc.tile_pool(name="gwpool", bufs=4))
        respool = ctx.enter_context(tc.tile_pool(name="respool", bufs=8))
        psum = ctx.enter_context(tc.psum_pool(name="psum", bufs=8))
        ctx.enter_context(tc.manual_schedule())

        graw = const.tile([P, NB], BF16, name="graw")
        nc.vector.memset(graw[:], 0.0)
        identb = const.tile([P, P], BF16, name="identb")
        make_identity(nc, identb[:])
        ident = const.tile([P, P], F32, name="ident")
        make_identity(nc, ident[:])
        eps = const.tile([P, 16], F32, name="eps")
        nc.vector.memset(eps[:], EPS)
        warm = const.tile([P, 16], F32, name="warm")
        nc.scalar.activation(out=warm[:], in_=eps[:], func=ACT.Abs_reciprocal_sqrt)
        junk = const.tile([P, E], BF16, name="junk")
        gb = const.tile([P, E], BF16, name="gb")
        hq = const.tile([P, 8, NB], U32, name="hq", align_bytes=64)
        hs = const.tile([P, 8, NB], U8, name="hs", align_bytes=64)
        wq = const.tile([P, 4, E], U32, name="wq", align_bytes=64)
        ws = const.tile([P, 4, E], U8, name="ws", align_bytes=64)

        xt = {}
        wt = {}
        for s in LOADS:
            n = int(s[1:])
            if s[0] == "x":
                t = xpool.tile([P, E], BF16, name="xt")
                if n == 0:
                    nc.sync.dma_start(out=t[:, 0:EH], in_=x[0:P, 0:EH])
                    nc.sync.dma_start(out=graw[0:4, :], in_=norm_query_w.rearrange("(c w) -> c w", w=NB))
                    nc.sync.dma_start(out=t[:, EH:E], in_=x[0:P, EH:E])
                else:
                    nc.sync.dma_start(out=t[:], in_=x[n * P:(n + 1) * P, :])
                xt[n] = t
            else:
                for a in range(4):
                    t = wpool.tile([P, E], BF16, name="wt")
                    wt[(n, a)] = t
                if n == 0:
                    for half in range(2):
                        for a in range(2):
                            nc.sync.dma_start(out=wt[(0, a)][:, half * EH:(half + 1) * EH],
                                              in_=W_in[a * P:(a + 1) * P, half * EH:(half + 1) * EH])
                for a in range(4):
                    if n > 0 or a >= 2:
                        r0 = n * NB + a * P
                        nc.sync.dma_start(out=wt[(n, a)][:], in_=W_in[r0:r0 + P, :])

        st = {}

        def gain():
            for c in range(4):
                gps = psum.tile([P, NB], BF16, name="gps", tag="ps")
                nc.tensor.matmul(gps[:], lhsT=identb[:, c:c + 1].to_broadcast([P, P]), rhs=graw[:], start=True, stop=True)
                nc.vector.tensor_copy(out=gb[:].rearrange("p (u c j e) -> p c u j e", u=2, c=4, e=2)[:, c],
                                      in_=gps[:].rearrange("p (j u e) -> p u j e", u=2, e=2))

        def stats(i):
            ss = small.tile([P, 1], F32, name="ss")
            rms = small.tile([P, 1], F32, name="rms")
            if i == 0:
                nc.scalar.activation(out=junk[:, 0:EH], in_=xt[i][:, 0:EH], func=ACT.Square, accum_out=ss[:])
                ss2 = const.tile([P, 1], F32, name="ss2")
                nc.scalar.activation(out=junk[:, EH:E], in_=xt[i][:, EH:E], func=ACT.Square, accum_out=ss2[:])
                part = const.tile([P, 1], F32, name="part")
                nc.scalar.activation(out=part[:], in_=ss2[:], func=ACT.Identity, bias=eps[:, 0:1], scale=1.0 / E)
                nc.scalar.activation(out=rms[:], in_=ss[:], func=ACT.Abs_reciprocal_sqrt, bias=part[:], scale=1.0 / E)
            else:
                nc.scalar.activation(out=junk[:], in_=xt[i][:], func=ACT.Square, accum_out=ss[:])
                nc.scalar.activation(out=rms[:], in_=ss[:], func=ACT.Abs_reciprocal_sqrt, bias=eps[:, 0:1], scale=1.0 / E)
            st[("rstd", i)] = rms

        def recip(i):
            h = hpool.tile([P, E], BF16, name="h")
            st[("h", i)] = h

        def scale(i, u):
            h = st[("h", i)]
            nc.vector.scalar_tensor_tensor(
                out=h[:, u * EH:(u + 1) * EH].rearrange("p (q e) -> p q e", e=2),
                in0=xt[i][:].rearrange("p (q u e) -> p u q e", u=2, e=2)[:, u],
                scalar=st[("rstd", i)][:, 0:1],
                in1=gb[:, u * EH:(u + 1) * EH].rearrange("p (q e) -> p q e", e=2),
                op0=ALU.mult, op1=ALU.mult)

        def trx(i):
            words = st[("h", i)][:].bitcast(F32)
            banks = []
            for k in range(2):
                bank = psum.tile([P, 2, 2, P], F32, name="xbank", tag="ps")
                banks.append(bank)
            for u in range(2):
                for k in range(2):
                    for v in range(2):
                        col = u * NB + (2 * k + v) * P
                        nc.tensor.transpose(banks[k][:, v, u, :], words[:, col:col + P], ident[:])
            st[("xb", i)] = banks
            st[("gh", i)] = ghpool.tile([P, 4, 4 * P], BF16, name="gh", align_bytes=64)

        def outx(i, k, engine):
            gh = st[("gh", i)]
            dst = gh[:, 2 * k:2 * k + 2, :].bitcast(F32).rearrange("p c (r u) -> p c r u", u=2)
            src = st[("xb", i)][k][:].rearrange("p c u r -> p c r u")
            if engine == "S":
                nc.scalar.copy(out=dst, in_=src)
            else:
                nc.vector.tensor_copy(out=dst, in_=src)

        def qx(i):
            nc.vector.quantize_mx(out=hq[:, i, :].bitcast(FP8X4), scales=hs[:, i, :],
                                  in_=st[("gh", i)][:].rearrange("p c w -> p (c w)"))

        def trw(j, h):
            banks = []
            for c in range(4):
                bank = psum.tile([P, 2, NH], F32, name="wbank", tag="ps")
                banks.append(bank)
            runs = [(a, c) for a in range(2) for c in range(4)]
            if (j, h) == (0, 0):
                runs = [(a, c) for c in range(4) for a in range(2)]
            for a, c in runs:
                for u in range(2):
                    w0 = c * NH + u
                    nc.tensor.transpose(banks[c][:, u, a * P:(a + 1) * P],
                                        wt[(j, 2 * h + a)][:].bitcast(F32)[:, w0:(c + 1) * NH:2], ident[:])
            st[("wb", j, h)] = banks

        def outw(j, h, engines, cs=(0, 1, 2, 3)):
            if cs[0] == 0:
                st[("gw", j, h)] = gwpool.tile([P, 4, 4 * NH], BF16, name="gw", align_bytes=64)
            gw = st[("gw", j, h)]
            for c in cs:
                dst = gw[:, c, :].bitcast(F32).rearrange("p (n u) -> p n u", u=2)
                src = st[("wb", j, h)][c][:].rearrange("p u n -> p n u")
                if engines[c] == "S":
                    nc.scalar.copy(out=dst, in_=src)
                else:
                    nc.vector.tensor_copy(out=dst, in_=src)

        def qw(j, h, cs=(0, 1, 2, 3)):
            n0 = j * NB + h * NH
            for c in cs:
                nc.vector.quantize_mx(out=wq[:, c, n0:n0 + NH].bitcast(FP8X4), scales=ws[:, c, n0:n0 + NH],
                                      in_=st[("gw", j, h)][:, c, :])

        def mm(i, j):
            acc = psum.tile([P, NB], F32, name="acc", tag="ps")
            for c in range(4):
                nc.tensor.matmul_mx(
                    out=acc[:],
                    lhsT=hq[:, i, c * P:(c + 1) * P].bitcast(FP8X4), lhsT_scale=hs[:, i, c * P:(c + 1) * P],
                    rhs=wq[:, c, j * NB:(j + 1) * NB].bitcast(FP8X4), rhs_scale=ws[:, c, j * NB:(j + 1) * NB],
                    start=(c == 0), stop=(c == 3))
            st[("acc", i, j)] = acc

        def mm2(i, ja, jb):
            accs = []
            for j in (ja, jb):
                acc = psum.tile([P, NB], F32, name="acc", tag="ps")
                st[("acc", i, j)] = acc
                accs.append(acc)
            for c in range(4):
                for acc, j in zip(accs, (ja, jb)):
                    nc.tensor.matmul_mx(
                        out=acc[:],
                        lhsT=hq[:, i, c * P:(c + 1) * P].bitcast(FP8X4), lhsT_scale=hs[:, i, c * P:(c + 1) * P],
                        rhs=wq[:, c, j * NB:(j + 1) * NB].bitcast(FP8X4), rhs_scale=ws[:, c, j * NB:(j + 1) * NB],
                        start=(c == 0), stop=(c == 3))

        def outc(i, j, engine):
            res = respool.tile([P, NB], F32, name="res")
            if engine == "S":
                nc.scalar.copy(out=res[:], in_=st[("acc", i, j)][:])
            else:
                nc.vector.tensor_copy(out=res[:], in_=st[("acc", i, j)][:])
            nc.sync.dma_start(out=o[i * P:(i + 1) * P, j * NB:(j + 1) * NB], in_=res[:])

        gain()
        stats(0)
        trw(0, 0)
        outw(0, 0, "SSSS")
        recip(0)
        scale(0, 0)
        scale(0, 1)
        trw(0, 1)
        outw(0, 1, "SSSS")
        qw(0, 0)
        trx(0)
        outx(0, 0, "V")
        outx(0, 1, "S")
        trw(1, 0)
        outw(1, 0, "VSSV", (0, 1))
        qw(0, 1)
        qx(0)
        outw(1, 0, "VSSV", (2, 3))
        trw(1, 1)
        mm(0, 0)
        outw(1, 1, "SVSV")
        qw(1, 0)
        stats(1)
        outc(0, 0, "S")
        trw(2, 0)
        outw(2, 0, "VSVS")
        recip(1)
        scale(1, 0)
        scale(1, 1)
        qw(1, 1)
        trw(2, 1)
        outw(2, 1, "SSSS")
        qw(2, 0)
        trw(3, 0)
        outw(3, 0, "SSSV")
        trx(1)
        outx(1, 0, "S")
        outx(1, 1, "V")
        qw(2, 1)
        qx(1)
        trw(3, 1)
        outw(3, 1, "SSSV")
        qw(3, 0)
        mm2(0, 1, 2)
        stats(2)
        qw(3, 1)
        outc(0, 1, "S")
        mm2(1, 0, 1)
        recip(2)
        scale(2, 0)
        outc(0, 2, "S")
        scale(2, 1)
        stats(3)
        mm(0, 3)
        outc(1, 0, "S")
        recip(3)
        scale(3, 0)
        outc(1, 1, "S")
        for i in range(2, 8):
            if i > 2:
                mm2(i - 1, 0, 1)
            trx(i)
            mm2(i - 1, 2, 3)
            if i > 2:
                outc(i - 2, 3, "V")
                outc(i - 1, 0, "S")
            if 2 < i < 7:
                recip(i + 1)
                scale(i + 1, 0)
            outx(i, 0, "S")
            outx(i, 1, "V")
            qx(i)
            if i < 7:
                scale(i + 1, 1)
            if i < 6:
                stats(i + 2)
            if i == 2:
                outc(0, 3, "S")
            else:
                outc(i - 1, 1, "S")
            outc(i - 1, 2, "S")
        outc(6, 3, "V")
        mm2(7, 0, 1)
        mm(7, 2)
        halves = []
        for h in range(2):
            acc = psum.tile([P, NH], F32, name="acch", tag="ps")
            n0 = 3 * NB + h * NH
            for c in range(4):
                nc.tensor.matmul_mx(
                    out=acc[:],
                    lhsT=hq[:, 7, c * P:(c + 1) * P].bitcast(FP8X4), lhsT_scale=hs[:, 7, c * P:(c + 1) * P],
                    rhs=wq[:, c, n0:n0 + NH].bitcast(FP8X4), rhs_scale=ws[:, c, n0:n0 + NH],
                    start=(c == 0), stop=(c == 3))
            halves.append(acc)
        for j in range(3):
            outc(7, j, "V" if j % 2 else "S")
        for h in range(2):
            res = respool.tile([P, NH], F32, name="resh", tag="res")
            if h == 0:
                nc.vector.tensor_copy(out=res[:], in_=halves[h][:])
            else:
                nc.scalar.copy(out=res[:], in_=halves[h][:])
            n0 = 3 * NB + h * NH
            nc.sync.dma_start(out=o[7 * P:8 * P, n0:n0 + NH], in_=res[:])
